import numpy as np
import ml_dtypes


def mxq(x, axis, fmt="e4m3"):
    dtype, down = {"e4m3": (ml_dtypes.float8_e4m3fn, 7), "e5m2": (ml_dtypes.float8_e5m2, 14)}[fmt]
    v = np.moveaxis(np.asarray(x, np.float32).astype(ml_dtypes.bfloat16).astype(np.float64), axis, -1)
    blocks = v.reshape(v.shape[:-1] + (-1, 32))
    amax = np.abs(blocks).max(-1, keepdims=True)
    byte = np.maximum(np.where(amax > 0, np.frexp(amax)[1] - 1 + 127, 0) - down, 1)
    scale = np.exp2(byte - 127.0)
    codes = (blocks / scale).astype(np.float32).astype(dtype).astype(np.float64)
    return np.moveaxis((codes * scale).reshape(v.shape), -1, axis)


WIDE = False


def mx_kscale(k):
    if not WIDE:
        return np.ones(k)
    levels = np.array([10, -10, 5, -5, 0])
    a = np.random.permutation(np.resize(levels, k // 512 * 4)).reshape(k // 512, 4)
    idx = np.arange(k)
    return np.exp2(a[idx // 512, idx % 128 // 32])


BF16 = ml_dtypes.bfloat16


def bf(x):
    return np.asarray(x, np.float32).astype(BF16)


def f64(x):
    return np.asarray(x).astype(np.float64)


E2M1 = np.array([0.0, 0.5, 1.0, 1.5, 2.0, 3.0, 4.0, 6.0, -0.0, -0.5, -1.0, -1.5, -2.0, -3.0, -4.0, -6.0])


def pack_weight(w, fmt):
    k, n = w.shape
    w = f64(bf(w)).reshape(k // 32, 32, n)
    amax = np.abs(w).max(1)
    if fmt == "e4m3":
        byte = np.frexp(amax)[1] - 1 + 127 - 7
    else:
        mant, ex = np.frexp(amax / 6.0)
        byte = np.where(mant > 0.5, ex, ex - 1) + 127
    byte = np.clip(np.where(amax > 0, byte, 1), 1, 254)
    scaled = (w * np.exp2(127.0 - byte)[:, None, :]).reshape(k, n).astype(np.float32)
    by_word = np.ascontiguousarray(scaled.reshape(k // 512, 128, 4, n).transpose(0, 1, 3, 2))
    if fmt == "e4m3":
        words = by_word.astype(ml_dtypes.float8_e4m3fn).view(np.uint8)
    else:
        c = by_word.astype(ml_dtypes.float4_e2m1fn).view(np.uint8) & 0xF
        words = c[..., 0::2] | (c[..., 1::2] << 4)
    return np.ascontiguousarray(words), np.ascontiguousarray(byte.astype(np.uint8).reshape(k // 512, 16, n))


def unpack_weight(words, scales, fmt):
    g, p, n, _ = words.shape
    if fmt == "e4m3":
        vals = np.ascontiguousarray(words).view(ml_dtypes.float8_e4m3fn).astype(np.float64)
    else:
        nib = np.empty((g, p, n, 4), np.uint8)
        nib[..., 0::2] = words & 0xF
        nib[..., 1::2] = words >> 4
        vals = E2M1[nib]
    vals = vals * np.repeat(np.exp2(scales.astype(np.float64) - 127.0), 8, axis=1)[..., None]
    return vals.transpose(0, 1, 3, 2).reshape(g * 512, n)


B, IN_CH, OUT_CH, KH, KW, H, W_IN = 2, 16, 4096, 4, 4, 11, 11
HO, WO = H - KH + 1, W_IN - KW + 1
L = HO * WO
KD = KH * KW
F = IN_CH * KD * KD
MXB = 32
FMT = "e4m3"


def setup_inputs():
    s = mx_kscale(F)[(np.arange(IN_CH) * KD * KD) // MXB * MXB]
    u = np.exp2(np.round(np.log2(s) / 2))
    x = bf(np.random.standard_normal((B, IN_CH, H, W_IN)) * u[None, :, None, None])
    w = np.random.standard_normal((OUT_CH, F)) / np.sqrt(F) / np.repeat(u * u, KD * KD)[None, :]
    words, scales = pack_weight(np.ascontiguousarray(w.T), FMT)
    return {"x": x, "W_words": words, "W_scales": scales}


def _unfold(x):
    patches = np.stack([x[:, :, i:i + HO, j:j + WO] for i in range(KH) for j in range(KW)], axis=2)
    return patches.reshape(B, IN_CH, KD, L).transpose(0, 3, 1, 2)


def reference(x, W_words, W_scales):
    p = _unfold(f64(x))
    outer = np.einsum("blci,blcj->blcij", p, p)
    feat = outer.reshape(B, L, F)
    out = unpack_weight(W_words, W_scales, FMT).T @ mxq(feat, 2, "e4m3").transpose(0, 2, 1)
    return out.reshape(B, OUT_CH, HO, WO)

@@ -1,0 +1,204 @@
+from contextlib import ExitStack
+
+import concourse.mybir as mybir
+from concourse.masks import make_identity
+
+BF16 = mybir.dt.bfloat16
+F32 = mybir.dt.float32
+I32 = mybir.dt.int32
+U32 = mybir.dt.uint32
+U8 = mybir.dt.uint8
+FP8X4 = mybir.dt.float8_e4m3fn_x4
+MULT = mybir.AluOpType.mult
+
+P = 128
+FLOPS = 2 * 128 * 4096 * 4096
+
+
+def tile_fast2order_de_conv_w_kernel(tc, x, W_words, W_scales, out):
+    nc = tc.nc
+    with ExitStack() as ctx:
+        ctx.enter_context(tc.manual_schedule())
+        const = ctx.enter_context(tc.tile_pool(name="const", bufs=1))
+        stage_s = ctx.enter_context(tc.tile_pool(name="stage_s", bufs=4))
+        stage_o = ctx.enter_context(tc.tile_pool(name="stage_o", bufs=8))
+        psum = ctx.enter_context(tc.psum_pool(name="psum", bufs=1))
+
+        x0 = const.tile([P, 164], BF16, name="x0")
+        planes = const.tile([P, 2, 4096], U8, name="planes", align_bytes=64)
+        ident_bf = const.tile([P, P], BF16, name="ident_bf")
+        ident_f = const.tile([P, P], F32, name="ident_f")
+        sel_a = const.tile([P, 512], BF16, name="sel_a")
+        sel_b = const.tile([P, 4, 512], BF16, name="sel_b")
+        pt_sb = const.tile([P, 512], BF16, name="pt_sb")
+        r_sb = const.tile([P, 256], BF16, name="r_sb")
+        a_sb = const.tile([P, 4, 256], BF16, name="a_sb")
+        grouped = const.tile([P, 4, 1024], BF16, name="grouped", align_bytes=64)
+        fw = const.tile([P, 4, 256], U32, name="fw", align_bytes=64)
+        fs = const.tile([P, 4, 256], U8, name="fs", align_bytes=64)
+
+        def copy_out(engine, dst, src):
+            if engine == 0:
+                nc.scalar.copy(out=dst, in_=src)
+            else:
+                nc.vector.tensor_copy(out=dst, in_=src)
+
+        nc.vector.memset(x0[:], 0.0)
+        nc.sync.dma_start(out=x0[0:32, 0:121], in_=x.rearrange("n c h w -> (n c) (h w)"))
+        nc.vector.memset(planes[:].bitcast(I32), 0)
+        make_identity(nc, ident_bf[:])
+        make_identity(nc, ident_f[:])
+        for h in range(2):
+            for q in range(4):
+                nc.sync.dma_start(
+                    out=planes[32 * q : 32 * q + 16, h, :].bitcast(I32),
+                    in_=W_scales[4 * h : 4 * h + 4, 4 * q : 4 * q + 4, :].bitcast(I32),
+                )
+
+        def load_w(g, o0, width, name):
+            w = const.tile([P, width], I32, name=name, align_bytes=64)
+            src = W_words[g].rearrange("p n t -> p (n t)")[:, 4 * o0 : 4 * (o0 + width)]
+            nc.sync.dma_start(out=w[:], in_=src.bitcast(I32))
+            return w
+
+        w_h0 = [load_w(g, 0, 2048, "w0_%d" % g) for g in range(8)]
+        w_h1 = [load_w(g, 2048, 2048, "w1_%d" % g) for g in range(7)]
+        w_last = [load_w(7, 2048 + 512 * j, 512, "w1_7_%d" % j) for j in range(4)]
+
+        nc.vector.tensor_copy(
+            out=sel_a[:].rearrange("q (v j) -> q v j", j=4),
+            in_=ident_bf[:].unsqueeze(2).to_broadcast([P, P, 4]),
+        )
+        ident_ajt = ident_bf[:].rearrange("q (a j t) -> q a j t", a=8, j=4, t=4)
+        for t in range(4):
+            nc.vector.tensor_copy(
+                out=sel_b[:, t, :].rearrange("q (a i j) -> q a i j", a=8, i=16, j=4),
+                in_=ident_ajt[:, :, :, t].unsqueeze(2).to_broadcast([P, 8, 16, 4]),
+            )
+
+        pt_view = pt_sb[:].rearrange("e (q i) -> e q i", i=16)
+        for half in range(2):
+            pt_ps = psum.tile([P, 8, P], BF16, name="pt_ps%d" % half, tag="b%d" % half)
+            for k in range(8):
+                i = 8 * half + k
+                off = (i // 4) * 11 + i % 4
+                nc.tensor.transpose(pt_ps[:, k, :], x0[:, off : off + P], ident_bf[:])
+            copy_out(
+                1,
+                pt_view[:, :, 8 * half : 8 * half + 8],
+                pt_ps[:, :, 0:32].rearrange("e i q -> e q i"),
+            )
+        r_ps = psum.tile([P, 4, P], BF16, name="r_ps", tag="b2")
+        for ghi in range(2):
+            for n in range(2):
+                s = (n * 16 + ghi * 8) * 16
+                nc.tensor.transpose(r_ps[:, ghi * 2 + n, :], pt_sb[:, s : s + P], ident_bf[:])
+        nc.vector.tensor_copy(
+            out=r_sb[:].rearrange("q (b y z) -> q b y z", b=4, y=8),
+            in_=r_ps[:, :, 0:88].rearrange("q b (y w) -> q b y w", w=11)[:, :, :, 0:8],
+        )
+
+        a_ps = psum.tile([P, 4, 256], BF16, name="a_ps", tag="b3")
+        for glo in range(4):
+            nc.tensor.matmul(
+                a_ps[:, glo, :], lhsT=sel_a[:, glo * P : (glo + 1) * P], rhs=r_sb[:],
+                start=True, stop=True,
+            )
+        nc.scalar.copy(out=a_sb[:], in_=a_ps[:])
+        b_ps = []
+        for glo in range(4):
+            b = psum.tile([P, 4, 256], BF16, name="b_ps%d" % glo, tag="b%d" % (4 + glo))
+            for t in range(4):
+                nc.tensor.matmul(
+                    b[:, t, :], lhsT=sel_b[:, t, glo * P : (glo + 1) * P], rhs=r_sb[:],
+                    start=True, stop=True,
+                )
+            b_ps.append(b)
+
+        def product(glo):
+            nc.vector.tensor_tensor(
+                out=grouped[:, glo, :].rearrange("p (c t) -> p c t", t=4),
+                in0=a_sb[:, glo, :].unsqueeze(2).to_broadcast([P, 256, 4]),
+                in1=b_ps[glo][:].rearrange("p t c -> p c t"),
+                op=MULT,
+            )
+
+        def quantise(glo):
+            nc.vector.quantize_mx(
+                out=fw[:, glo, :].bitcast(FP8X4), scales=fs[:, glo, :], in_=grouped[:, glo, :]
+            )
+
+        product(0)
+        product(1)
+        quantise(0)
+        product(2)
+        quantise(1)
+        product(3)
+        quantise(2)
+        quantise(3)
+
+        def mx_pass(acc, g, w_cols, o0):
+            ghi, glo = g // 4, g % 4
+            nc.tensor.matmul_mx(
+                out=acc[:],
+                lhsT=fw[:, glo, ghi * P : (ghi + 1) * P].bitcast(FP8X4),
+                lhsT_scale=fs[:, glo, ghi * P : (ghi + 1) * P],
+                rhs=w_cols.bitcast(FP8X4),
+                rhs_scale=planes[4 * glo : P, ghi, o0 : o0 + 512],
+                start=(g == 0),
+                stop=(g == 7),
+            )
+
+        out_rows = out.rearrange("n o y z -> n o (y z)")
+
+        def evac1(acc, engine):
+            s = stage_s.tile([P, 4, P], F32, name="s", tag="s")
+            copy_out(engine, s[:], acc[:].rearrange("p (m r) -> p r m", r=4))
+            return s
+
+        def back(s, bank):
+            t_ps = psum.tile([P, 4, P], F32, name="t_ps", tag="b%d" % bank)
+            for r in range(4):
+                nc.tensor.transpose(t_ps[:, r, :], s[:, r, :], ident_f[:])
+            return t_ps
+
+        def evac2_store(t_ps, engine, o0):
+            o_sb = stage_o.tile([P, 2, 4, 64], F32, name="o_sb", tag="o")
+            copy_out(engine, o_sb[:], t_ps[:].rearrange("m r (n l) -> m n r l", n=2))
+            nc.sync.dma_start(
+                out=out_rows[:, o0 : o0 + 512, :].rearrange("n (m r) l -> m n (r l)", r=4),
+                in_=o_sb[:].rearrange("m n r l -> m n (r l)"),
+            )
+
+        acc0 = [psum.tile([P, 512], F32, name="acc0_%d" % j, tag="b%d" % j) for j in range(4)]
+        for g in range(8):
+            for j in range(4):
+                mx_pass(acc0[j], g, w_h0[g][:, 512 * j : 512 * (j + 1)], 512 * j)
+        s0 = [evac1(acc0[j], j % 2) for j in range(4)]
+        t0 = [back(s0[j], j) for j in range(4)]
+        for j in range(4):
+            evac2_store(t0[j], j % 2, 512 * j)
+
+        acc1 = [psum.tile([P, 512], F32, name="acc1_%d" % j, tag="b%d" % (4 + j)) for j in range(4)]
+        for g in range(7):
+            for j in range(4):
+                mx_pass(acc1[j], g, w_h1[g][:, 512 * j : 512 * (j + 1)], 2048 + 512 * j)
+        s1 = [None] * 4
+        t1 = [None] * 4
+
+        def close(j):
+            mx_pass(acc1[j], 7, w_last[j][:], 2048 + 512 * j)
+            s1[j] = evac1(acc1[j], j % 2)
+
+        def finish(j):
+            t1[j] = back(s1[j], j)
+            evac2_store(t1[j], (j + 1) % 2, 2048 + 512 * j)
+
+        close(0)
+        close(1)
+        finish(0)
+        close(2)
+        finish(1)
+        close(3)
+        finish(2)
+        finish(3)

@@ -20,8 +20,8 @@ def tile_fast2order_de_conv_w_kernel(tc, x, W_words, W_scales, out):
     with ExitStack() as ctx:
         ctx.enter_context(tc.manual_schedule())
         const = ctx.enter_context(tc.tile_pool(name="const", bufs=1))
-        stage_s = ctx.enter_context(tc.tile_pool(name="stage_s", bufs=4))
-        stage_o = ctx.enter_context(tc.tile_pool(name="stage_o", bufs=8))
+        stage_s = ctx.enter_context(tc.tile_pool(name="stage_s", bufs=3))
+        stage_o = ctx.enter_context(tc.tile_pool(name="stage_o", bufs=4))
         psum = ctx.enter_context(tc.psum_pool(name="psum", bufs=1))
 
         x0 = const.tile([P, 164], BF16, name="x0")
@@ -44,16 +44,16 @@ def tile_fast2order_de_conv_w_kernel(tc, x, W_words, W_scales, out):
                 nc.vector.tensor_copy(out=dst, in_=src)
 
         nc.vector.memset(x0[:], 0.0)
-        nc.sync.dma_start(out=x0[0:32, 0:121], in_=x.rearrange("n c h w -> (n c) (h w)"))
+        nc.scalar.dma_start(out=x0[0:32, 0:121], in_=x.rearrange("n c h w -> (n c) (h w)"))
         nc.vector.memset(planes[:].bitcast(I32), 0)
         make_identity(nc, ident_bf[:])
-        make_identity(nc, ident_f[:])
         for h in range(2):
             for q in range(4):
                 nc.sync.dma_start(
                     out=planes[32 * q : 32 * q + 16, h, :].bitcast(I32),
                     in_=W_scales[4 * h : 4 * h + 4, 4 * q : 4 * q + 4, :].bitcast(I32),
                 )
+        make_identity(nc, ident_f[:])
 
         def load_w(g, o0, width, name):
             w = const.tile([P, width], I32, name=name, align_bytes=64)
@@ -61,9 +61,8 @@ def tile_fast2order_de_conv_w_kernel(tc, x, W_words, W_scales, out):
             nc.sync.dma_start(out=w[:], in_=src.bitcast(I32))
             return w
 
-        w_h0 = [load_w(g, 0, 2048, "w0_%d" % g) for g in range(8)]
-        w_h1 = [load_w(g, 2048, 2048, "w1_%d" % g) for g in range(7)]
-        w_last = [load_w(7, 2048 + 512 * j, 512, "w1_7_%d" % j) for j in range(4)]
+        w_full = [load_w(g, 0, 4096, "w_%d" % g) for g in range(7)]
+        w_last = [load_w(7, 1024 * c, 1024, "w_7_%d" % c) for c in range(4)]
 
         nc.vector.tensor_copy(
             out=sel_a[:].rearrange("q (v j) -> q v j", j=4),
@@ -150,49 +149,45 @@ def tile_fast2order_de_conv_w_kernel(tc, x, W_words, W_scales, out):
             )
 
         out_rows = out.rearrange("n o y z -> n o (y z)")
+        acc = [psum.tile([P, 512], F32, name="acc%d" % j, tag="b%d" % j) for j in range(8)]
+        for g in range(7):
+            for j in range(8):
+                mx_pass(acc[j], g, w_full[g][:, 512 * j : 512 * (j + 1)], 512 * j)
 
-        def evac1(acc, engine):
-            s = stage_s.tile([P, 4, P], F32, name="s", tag="s")
-            copy_out(engine, s[:], acc[:].rearrange("p (m r) -> p r m", r=4))
-            return s
+        s_tiles = [None] * 4
 
-        def back(s, bank):
-            t_ps = psum.tile([P, 4, P], F32, name="t_ps", tag="b%d" % bank)
-            for r in range(4):
-                nc.tensor.transpose(t_ps[:, r, :], s[:, r, :], ident_f[:])
-            return t_ps
+        def close(c):
+            s = stage_s.tile([P, 8, P], F32, name="s", tag="s")
+            for a in range(2):
+                j = 2 * c + a
+                mx_pass(acc[j], 7, w_last[c][:, 512 * a : 512 * (a + 1)], 512 * j)
+            for a in range(2):
+                copy_out(
+                    a,
+                    s[:, :, 64 * a : 64 * (a + 1)],
+                    acc[2 * c + a][:].rearrange("p (m r) -> p r m", r=8),
+                )
+            s_tiles[c] = s
 
-        def evac2_store(t_ps, engine, o0):
-            o_sb = stage_o.tile([P, 2, 4, 64], F32, name="o_sb", tag="o")
-            copy_out(engine, o_sb[:], t_ps[:].rearrange("m r (n l) -> m n r l", n=2))
+        def finish(c):
+            s = s_tiles[c]
+            o_sb = stage_o.tile([P, 2, 8, 64], F32, name="o_sb", tag="o")
+            t_ps = []
+            for a in range(2):
+                t = psum.tile([P, 4, P], F32, name="t_ps", tag="b%d" % (2 * c + a))
+                for r in range(4):
+                    nc.tensor.transpose(t[:, r, :], s[:, 4 * a + r, :], ident_f[:])
+                t_ps.append(t)
+            for a in range(2):
+                copy_out(
+                    a,
+                    o_sb[:, :, 4 * a : 4 * (a + 1), :],
+                    t_ps[a][:].rearrange("m r (n l) -> m n r l", n=2),
+                )
             nc.sync.dma_start(
-                out=out_rows[:, o0 : o0 + 512, :].rearrange("n (m r) l -> m n (r l)", r=4),
+                out=out_rows[:, 1024 * c : 1024 * (c + 1), :].rearrange("n (m r) l -> m n (r l)", r=8),
                 in_=o_sb[:].rearrange("m n r l -> m n (r l)"),
             )
-
-        acc0 = [psum.tile([P, 512], F32, name="acc0_%d" % j, tag="b%d" % j) for j in range(4)]
-        for g in range(8):
-            for j in range(4):
-                mx_pass(acc0[j], g, w_h0[g][:, 512 * j : 512 * (j + 1)], 512 * j)
-        s0 = [evac1(acc0[j], j % 2) for j in range(4)]
-        t0 = [back(s0[j], j) for j in range(4)]
-        for j in range(4):
-            evac2_store(t0[j], j % 2, 512 * j)
-
-        acc1 = [psum.tile([P, 512], F32, name="acc1_%d" % j, tag="b%d" % (4 + j)) for j in range(4)]
-        for g in range(7):
-            for j in range(4):
-                mx_pass(acc1[j], g, w_h1[g][:, 512 * j : 512 * (j + 1)], 2048 + 512 * j)
-        s1 = [None] * 4
-        t1 = [None] * 4
-
-        def close(j):
-            mx_pass(acc1[j], 7, w_last[j][:], 2048 + 512 * j)
-            s1[j] = evac1(acc1[j], j % 2)
-
-        def finish(j):
-            t1[j] = back(s1[j], j)
-            evac2_store(t1[j], (j + 1) % 2, 2048 + 512 * j)
 
         close(0)
         close(1)

@@ -20,8 +20,8 @@ def tile_fast2order_de_conv_w_kernel(tc, x, W_words, W_scales, out):
     with ExitStack() as ctx:
         ctx.enter_context(tc.manual_schedule())
         const = ctx.enter_context(tc.tile_pool(name="const", bufs=1))
-        stage_s = ctx.enter_context(tc.tile_pool(name="stage_s", bufs=3))
-        stage_o = ctx.enter_context(tc.tile_pool(name="stage_o", bufs=4))
+        stage_s = ctx.enter_context(tc.tile_pool(name="stage_s", bufs=4))
+        stage_o = ctx.enter_context(tc.tile_pool(name="stage_o", bufs=8))
         psum = ctx.enter_context(tc.psum_pool(name="psum", bufs=1))
 
         x0 = const.tile([P, 164], BF16, name="x0")
@@ -47,13 +47,6 @@ def tile_fast2order_de_conv_w_kernel(tc, x, W_words, W_scales, out):
         nc.scalar.dma_start(out=x0[0:32, 0:121], in_=x.rearrange("n c h w -> (n c) (h w)"))
         nc.vector.memset(planes[:].bitcast(I32), 0)
         make_identity(nc, ident_bf[:])
-        for h in range(2):
-            for q in range(4):
-                nc.sync.dma_start(
-                    out=planes[32 * q : 32 * q + 16, h, :].bitcast(I32),
-                    in_=W_scales[4 * h : 4 * h + 4, 4 * q : 4 * q + 4, :].bitcast(I32),
-                )
-        make_identity(nc, ident_f[:])
 
         def load_w(g, o0, width, name):
             w = const.tile([P, width], I32, name=name, align_bytes=64)
@@ -61,8 +54,23 @@ def tile_fast2order_de_conv_w_kernel(tc, x, W_words, W_scales, out):
             nc.sync.dma_start(out=w[:], in_=src.bitcast(I32))
             return w
 
-        w_full = [load_w(g, 0, 4096, "w_%d" % g) for g in range(7)]
-        w_last = [load_w(7, 1024 * c, 1024, "w_7_%d" % c) for c in range(4)]
+        w_h0 = [load_w(0, 0, 2048, "w0_0")]
+        for h in range(2):
+            for q in range(2):
+                nc.sync.dma_start(
+                    out=planes[32 * q : 32 * q + 16, h, :].bitcast(I32),
+                    in_=W_scales[4 * h : 4 * h + 4, 4 * q : 4 * q + 4, :].bitcast(I32),
+                )
+        for r in range(4):
+            for q in range(2, 4):
+                nc.gpsimd.dma_start(
+                    out=planes[32 * q + r : 32 * q + 16 : 4, :, :].bitcast(F32),
+                    in_=W_scales[:, 4 * q + r, :].rearrange("(h k) n -> k h n", k=4).bitcast(F32),
+                )
+        make_identity(nc, ident_f[:])
+        w_h0.extend([load_w(g, 0, 2048, "w0_%d" % g) for g in range(1, 8)])
+        w_h1 = [load_w(g, 2048, 2048, "w1_%d" % g) for g in range(7)]
+        w_last = [load_w(7, 2048 + 512 * j, 512, "w1_7_%d" % j) for j in range(4)]
 
         nc.vector.tensor_copy(
             out=sel_a[:].rearrange("q (v j) -> q v j", j=4),
@@ -149,45 +157,49 @@ def tile_fast2order_de_conv_w_kernel(tc, x, W_words, W_scales, out):
             )
 
         out_rows = out.rearrange("n o y z -> n o (y z)")
-        acc = [psum.tile([P, 512], F32, name="acc%d" % j, tag="b%d" % j) for j in range(8)]
-        for g in range(7):
-            for j in range(8):
-                mx_pass(acc[j], g, w_full[g][:, 512 * j : 512 * (j + 1)], 512 * j)
 
-        s_tiles = [None] * 4
+        def evac1(acc, engine):
+            s = stage_s.tile([P, 4, P], F32, name="s", tag="s")
+            copy_out(engine, s[:], acc[:].rearrange("p (m r) -> p r m", r=4))
+            return s
 
-        def close(c):
-            s = stage_s.tile([P, 8, P], F32, name="s", tag="s")
-            for a in range(2):
-                j = 2 * c + a
-                mx_pass(acc[j], 7, w_last[c][:, 512 * a : 512 * (a + 1)], 512 * j)
-            for a in range(2):
-                copy_out(
-                    a,
-                    s[:, :, 64 * a : 64 * (a + 1)],
-                    acc[2 * c + a][:].rearrange("p (m r) -> p r m", r=8),
-                )
-            s_tiles[c] = s
+        def back(s, bank):
+            t_ps = psum.tile([P, 4, P], F32, name="t_ps", tag="b%d" % bank)
+            for r in range(4):
+                nc.tensor.transpose(t_ps[:, r, :], s[:, r, :], ident_f[:])
+            return t_ps
 
-        def finish(c):
-            s = s_tiles[c]
-            o_sb = stage_o.tile([P, 2, 8, 64], F32, name="o_sb", tag="o")
-            t_ps = []
-            for a in range(2):
-                t = psum.tile([P, 4, P], F32, name="t_ps", tag="b%d" % (2 * c + a))
-                for r in range(4):
-                    nc.tensor.transpose(t[:, r, :], s[:, 4 * a + r, :], ident_f[:])
-                t_ps.append(t)
-            for a in range(2):
-                copy_out(
-                    a,
-                    o_sb[:, :, 4 * a : 4 * (a + 1), :],
-                    t_ps[a][:].rearrange("m r (n l) -> m n r l", n=2),
-                )
+        def evac2_store(t_ps, engine, o0):
+            o_sb = stage_o.tile([P, 2, 4, 64], F32, name="o_sb", tag="o")
+            copy_out(engine, o_sb[:], t_ps[:].rearrange("m r (n l) -> m n r l", n=2))
             nc.sync.dma_start(
-                out=out_rows[:, 1024 * c : 1024 * (c + 1), :].rearrange("n (m r) l -> m n (r l)", r=8),
+                out=out_rows[:, o0 : o0 + 512, :].rearrange("n (m r) l -> m n (r l)", r=4),
                 in_=o_sb[:].rearrange("m n r l -> m n (r l)"),
             )
+
+        acc0 = [psum.tile([P, 512], F32, name="acc0_%d" % j, tag="b%d" % j) for j in range(4)]
+        for g in range(8):
+            for j in range(4):
+                mx_pass(acc0[j], g, w_h0[g][:, 512 * j : 512 * (j + 1)], 512 * j)
+        s0 = [evac1(acc0[j], j % 2) for j in range(4)]
+        t0 = [back(s0[j], j) for j in range(4)]
+        for j in range(4):
+            evac2_store(t0[j], j % 2, 512 * j)
+
+        acc1 = [psum.tile([P, 512], F32, name="acc1_%d" % j, tag="b%d" % (4 + j)) for j in range(4)]
+        for g in range(7):
+            for j in range(4):
+                mx_pass(acc1[j], g, w_h1[g][:, 512 * j : 512 * (j + 1)], 2048 + 512 * j)
+        s1 = [None] * 4
+        t1 = [None] * 4
+
+        def close(j):
+            mx_pass(acc1[j], 7, w_last[j][:], 2048 + 512 * j)
+            s1[j] = evac1(acc1[j], j % 2)
+
+        def finish(j):
+            t1[j] = back(s1[j], j)
+            evac2_store(t1[j], (j + 1) % 2, 2048 + 512 * j)
 
         close(0)
         close(1)

@@ -13,6 +13,7 @@ MULT = mybir.AluOpType.mult
 
 P = 128
 FLOPS = 2 * 128 * 4096 * 4096
+TAIL_G = 5
 
 
 def tile_fast2order_de_conv_w_kernel(tc, x, W_words, W_scales, out):
@@ -69,8 +70,16 @@ def tile_fast2order_de_conv_w_kernel(tc, x, W_words, W_scales, out):
                 )
         make_identity(nc, ident_f[:])
         w_h0.extend([load_w(g, 0, 2048, "w0_%d" % g) for g in range(1, 8)])
-        w_h1 = [load_w(g, 2048, 2048, "w1_%d" % g) for g in range(7)]
-        w_last = [load_w(7, 2048 + 512 * j, 512, "w1_7_%d" % j) for j in range(4)]
+        w_h1 = [load_w(g, 2048, 2048, "w1_%d" % g) for g in range(TAIL_G)]
+
+        def load_tail(j):
+            o0 = 2048 + 512 * j
+            w = const.tile([P, 8 - TAIL_G, 512], I32, name="w1_tail_%d" % j, align_bytes=64)
+            src = W_words[TAIL_G:8].rearrange("g p n t -> p g (n t)")[:, :, 4 * o0 : 4 * (o0 + 512)]
+            nc.sync.dma_start(out=w[:], in_=src.bitcast(I32))
+            return w
+
+        w_last = [load_tail(j) for j in range(4)]
 
         nc.vector.tensor_copy(
             out=sel_a[:].rearrange("q (v j) -> q v j", j=4),
@@ -187,14 +196,15 @@ def tile_fast2order_de_conv_w_kernel(tc, x, W_words, W_scales, out):
             evac2_store(t0[j], j % 2, 512 * j)
 
         acc1 = [psum.tile([P, 512], F32, name="acc1_%d" % j, tag="b%d" % (4 + j)) for j in range(4)]
-        for g in range(7):
+        for g in range(TAIL_G):
             for j in range(4):
                 mx_pass(acc1[j], g, w_h1[g][:, 512 * j : 512 * (j + 1)], 2048 + 512 * j)
         s1 = [None] * 4
         t1 = [None] * 4
 
         def close(j):
-            mx_pass(acc1[j], 7, w_last[j][:], 2048 + 512 * j)
+            for g in range(TAIL_G, 8):
+                mx_pass(acc1[j], g, w_last[j][:, g - TAIL_G, :], 2048 + 512 * j)
             s1[j] = evac1(acc1[j], j % 2)
 
         def finish(j):

@@ -26,7 +26,7 @@ def tile_fast2order_de_conv_w_kernel(tc, x, W_words, W_scales, out):
         psum = ctx.enter_context(tc.psum_pool(name="psum", bufs=1))
 
         x0 = const.tile([P, 164], BF16, name="x0")
-        planes = const.tile([P, 2, 4096], U8, name="planes", align_bytes=64)
+        planes = const.tile([P, 2, 4096], U8, name="planes", align_bytes=256)
         ident_bf = const.tile([P, P], BF16, name="ident_bf")
         ident_f = const.tile([P, P], F32, name="ident_f")
         sel_a = const.tile([P, 512], BF16, name="sel_a")
@@ -34,9 +34,9 @@ def tile_fast2order_de_conv_w_kernel(tc, x, W_words, W_scales, out):
         pt_sb = const.tile([P, 512], BF16, name="pt_sb")
         r_sb = const.tile([P, 256], BF16, name="r_sb")
         a_sb = const.tile([P, 4, 256], BF16, name="a_sb")
-        grouped = const.tile([P, 4, 1024], BF16, name="grouped", align_bytes=64)
-        fw = const.tile([P, 4, 256], U32, name="fw", align_bytes=64)
-        fs = const.tile([P, 4, 256], U8, name="fs", align_bytes=64)
+        grouped = const.tile([P, 4, 1024], BF16, name="grouped", align_bytes=256)
+        fw = const.tile([P, 4, 256], U32, name="fw", align_bytes=256)
+        fs = const.tile([P, 4, 256], U8, name="fs", align_bytes=256)
 
         def copy_out(engine, dst, src):
             if engine == 0:
@@ -50,7 +50,7 @@ def tile_fast2order_de_conv_w_kernel(tc, x, W_words, W_scales, out):
         make_identity(nc, ident_bf[:])
 
         def load_w(g, o0, width, name):
-            w = const.tile([P, width], I32, name=name, align_bytes=64)
+            w = const.tile([P, width], I32, name=name, align_bytes=256)
             src = W_words[g].rearrange("p n t -> p (n t)")[:, 4 * o0 : 4 * (o0 + width)]
             nc.sync.dma_start(out=w[:], in_=src.bitcast(I32))
             return w
@@ -74,7 +74,7 @@ def tile_fast2order_de_conv_w_kernel(tc, x, W_words, W_scales, out):
 
         def load_tail(j):
             o0 = 2048 + 512 * j
-            w = const.tile([P, 8 - TAIL_G, 512], I32, name="w1_tail_%d" % j, align_bytes=64)
+            w = const.tile([P, 8 - TAIL_G, 512], I32, name="w1_tail_%d" % j, align_bytes=256)
             src = W_words[TAIL_G:8].rearrange("g p n t -> p g (n t)")[:, :, 4 * o0 : 4 * (o0 + 512)]
             nc.sync.dma_start(out=w[:], in_=src.bitcast(I32))
             return w

@@ -14,6 +14,9 @@ MULT = mybir.AluOpType.mult
 P = 128
 FLOPS = 2 * 128 * 4096 * 4096
 TAIL_G = 5
+BLOCKS = [(0, 512), (512, 512), (1024, 512), (1536, 256), (1792, 256)]
+ACC_BANK = [4, 5, 6, 7, 0]
+BACK_BANK = [1, 2, 3, 1, 2]
 
 
 def tile_fast2order_de_conv_w_kernel(tc, x, W_words, W_scales, out):
@@ -69,17 +72,26 @@ def tile_fast2order_de_conv_w_kernel(tc, x, W_words, W_scales, out):
                     in_=W_scales[:, 4 * q + r, :].rearrange("(h k) n -> k h n", k=4).bitcast(F32),
                 )
         make_identity(nc, ident_f[:])
-        w_h0.extend([load_w(g, 0, 2048, "w0_%d" % g) for g in range(1, 8)])
+        w_h0.extend([load_w(g, 0, 2048, "w0_%d" % g) for g in range(1, 4)])
+
+        def load_pair(g):
+            w = const.tile([P, 2, 2048], I32, name="w0_%d_%d" % (g, g + 1), align_bytes=256)
+            src = W_words[g : g + 2].rearrange("g p n t -> p g (n t)")[:, :, 0 : 4 * 2048]
+            nc.sync.dma_start(out=w[:], in_=src.bitcast(I32))
+            return [w[:, 0, :], w[:, 1, :]]
+
+        w_h0.extend(load_pair(4))
+        w_h0.extend(load_pair(6))
         w_h1 = [load_w(g, 2048, 2048, "w1_%d" % g) for g in range(TAIL_G)]
 
-        def load_tail(j):
-            o0 = 2048 + 512 * j
-            w = const.tile([P, 8 - TAIL_G, 512], I32, name="w1_tail_%d" % j, align_bytes=256)
-            src = W_words[TAIL_G:8].rearrange("g p n t -> p g (n t)")[:, :, 4 * o0 : 4 * (o0 + 512)]
+        def load_tail(i):
+            o0, width = 2048 + BLOCKS[i][0], BLOCKS[i][1]
+            w = const.tile([P, 8 - TAIL_G, width], I32, name="w1_tail_%d" % i, align_bytes=256)
+            src = W_words[TAIL_G:8].rearrange("g p n t -> p g (n t)")[:, :, 4 * o0 : 4 * (o0 + width)]
             nc.sync.dma_start(out=w[:], in_=src.bitcast(I32))
             return w
 
-        w_last = [load_tail(j) for j in range(4)]
+        w_last = [load_tail(i) for i in range(len(BLOCKS))]
 
         nc.vector.tensor_copy(
             out=sel_a[:].rearrange("q (v j) -> q v j", j=4),
@@ -153,36 +165,36 @@ def tile_fast2order_de_conv_w_kernel(tc, x, W_words, W_scales, out):
         quantise(2)
         quantise(3)
 
-        def mx_pass(acc, g, w_cols, o0):
+        def mx_pass(acc, g, w_cols, o0, width=512):
             ghi, glo = g // 4, g % 4
             nc.tensor.matmul_mx(
                 out=acc[:],
                 lhsT=fw[:, glo, ghi * P : (ghi + 1) * P].bitcast(FP8X4),
                 lhsT_scale=fs[:, glo, ghi * P : (ghi + 1) * P],
                 rhs=w_cols.bitcast(FP8X4),
-                rhs_scale=planes[4 * glo : P, ghi, o0 : o0 + 512],
+                rhs_scale=planes[4 * glo : P, ghi, o0 : o0 + width],
                 start=(g == 0),
                 stop=(g == 7),
             )
 
         out_rows = out.rearrange("n o y z -> n o (y z)")
 
-        def evac1(acc, engine):
-            s = stage_s.tile([P, 4, P], F32, name="s", tag="s")
-            copy_out(engine, s[:], acc[:].rearrange("p (m r) -> p r m", r=4))
+        def evac1(acc, engine, R):
+            s = stage_s.tile([P, R, P], F32, name="s", tag="s", align_bytes=256)
+            copy_out(engine, s[:], acc[:].rearrange("p (m r) -> p r m", r=R))
             return s
 
-        def back(s, bank):
-            t_ps = psum.tile([P, 4, P], F32, name="t_ps", tag="b%d" % bank)
-            for r in range(4):
+        def back(s, bank, R):
+            t_ps = psum.tile([P, R, P], F32, name="t_ps", tag="b%d" % bank)
+            for r in range(R):
                 nc.tensor.transpose(t_ps[:, r, :], s[:, r, :], ident_f[:])
             return t_ps
 
-        def evac2_store(t_ps, engine, o0):
-            o_sb = stage_o.tile([P, 2, 4, 64], F32, name="o_sb", tag="o")
+        def evac2_store(t_ps, engine, o0, R):
+            o_sb = stage_o.tile([P, 2, R, 64], F32, name="o_sb", tag="o", align_bytes=256)
             copy_out(engine, o_sb[:], t_ps[:].rearrange("m r (n l) -> m n r l", n=2))
             nc.sync.dma_start(
-                out=out_rows[:, o0 : o0 + 512, :].rearrange("n (m r) l -> m n (r l)", r=4),
+                out=out_rows[:, o0 : o0 + P * R, :].rearrange("n (m r) l -> m n (r l)", r=R),
                 in_=o_sb[:].rearrange("m n r l -> m n (r l)"),
             )
 
@@ -190,32 +202,54 @@ def tile_fast2order_de_conv_w_kernel(tc, x, W_words, W_scales, out):
         for g in range(8):
             for j in range(4):
                 mx_pass(acc0[j], g, w_h0[g][:, 512 * j : 512 * (j + 1)], 512 * j)
-        s0 = [evac1(acc0[j], j % 2) for j in range(4)]
-        t0 = [back(s0[j], j) for j in range(4)]
+        s_all = const.tile([P, 16, P], F32, name="s_all")
         for j in range(4):
-            evac2_store(t0[j], j % 2, 512 * j)
+            copy_out(
+                j % 2,
+                s_all[:, :, 32 * j : 32 * (j + 1)],
+                acc0[j][:].rearrange("p (m r) -> p r m", r=16),
+            )
+        o_all = const.tile([P, 2, 16, 64], F32, name="o_all", align_bytes=256)
+        t0 = []
+        for b in range(4):
+            t_ps = psum.tile([P, 4, P], F32, name="t0_ps", tag="b%d" % b)
+            for r in range(4):
+                nc.tensor.transpose(t_ps[:, r, :], s_all[:, 4 * b + r, :], ident_f[:])
+            t0.append(t_ps)
+        for b in range(4):
+            copy_out(
+                b % 2,
+                o_all[:, :, 4 * b : 4 * (b + 1), :],
+                t0[b][:].rearrange("m r (n l) -> m n r l", n=2),
+            )
+        nc.sync.dma_start(
+            out=out_rows[:, 0:2048, :].rearrange("n (m r) l -> m n (r l)", r=16),
+            in_=o_all[:].rearrange("m n r l -> m n (r l)"),
+        )
 
-        acc1 = [psum.tile([P, 512], F32, name="acc1_%d" % j, tag="b%d" % (4 + j)) for j in range(4)]
+        acc1 = [
+            psum.tile([P, BLOCKS[i][1]], F32, name="acc1_%d" % i, tag="b%d" % ACC_BANK[i])
+            for i in range(len(BLOCKS))
+        ]
         for g in range(TAIL_G):
-            for j in range(4):
-                mx_pass(acc1[j], g, w_h1[g][:, 512 * j : 512 * (j + 1)], 2048 + 512 * j)
-        s1 = [None] * 4
-        t1 = [None] * 4
+            for i in range(len(BLOCKS)):
+                c0, width = BLOCKS[i]
+                mx_pass(acc1[i], g, w_h1[g][:, c0 : c0 + width], 2048 + c0, width)
+        s1 = [None] * len(BLOCKS)
 
-        def close(j):
+        def close(i):
+            c0, width = BLOCKS[i]
             for g in range(TAIL_G, 8):
-                mx_pass(acc1[j], g, w_last[j][:, g - TAIL_G, :], 2048 + 512 * j)
-            s1[j] = evac1(acc1[j], j % 2)
+                mx_pass(acc1[i], g, w_last[i][:, g - TAIL_G, :], 2048 + c0, width)
+            s1[i] = evac1(acc1[i], i % 2, width // P)
 
-        def finish(j):
-            t1[j] = back(s1[j], j)
-            evac2_store(t1[j], (j + 1) % 2, 2048 + 512 * j)
+        def finish(i):
+            c0, width = BLOCKS[i]
+            t_ps = back(s1[i], BACK_BANK[i], width // P)
+            evac2_store(t_ps, (i + 1) % 2, 2048 + c0, width // P)
 
         close(0)
-        close(1)
-        finish(0)
-        close(2)
-        finish(1)
-        close(3)
-        finish(2)
-        finish(3)
+        for i in range(1, len(BLOCKS)):
+            close(i)
+            finish(i - 1)
+        finish(len(BLOCKS) - 1)

from contextlib import ExitStack

import concourse.mybir as mybir
from concourse.masks import make_identity

BF16 = mybir.dt.bfloat16
F32 = mybir.dt.float32
I32 = mybir.dt.int32
U32 = mybir.dt.uint32
U8 = mybir.dt.uint8
FP8X4 = mybir.dt.float8_e4m3fn_x4
MULT = mybir.AluOpType.mult

P = 128
FLOPS = 2 * 128 * 4096 * 4096
TAIL_G = 5
BLOCKS = [(0, 512), (512, 512), (1024, 512), (1536, 256), (1792, 256)]
ACC_BANK = [4, 5, 6, 7, 0]
BACK_BANK = [1, 2, 3, 1, 2]


def tile_fast2order_de_conv_w_kernel(tc, x, W_words, W_scales, out):
    nc = tc.nc
    with ExitStack() as ctx:
        ctx.enter_context(tc.manual_schedule())
        const = ctx.enter_context(tc.tile_pool(name="const", bufs=1))
        stage_s = ctx.enter_context(tc.tile_pool(name="stage_s", bufs=4))
        stage_o = ctx.enter_context(tc.tile_pool(name="stage_o", bufs=8))
        psum = ctx.enter_context(tc.psum_pool(name="psum", bufs=1))

        x0 = const.tile([P, 164], BF16, name="x0")
        planes = const.tile([P, 2, 4096], U8, name="planes", align_bytes=256)
        ident_bf = const.tile([P, P], BF16, name="ident_bf")
        ident_f = const.tile([P, P], F32, name="ident_f")
        sel_a = const.tile([P, 512], BF16, name="sel_a")
        sel_b = const.tile([P, 4, 512], BF16, name="sel_b")
        pt_sb = const.tile([P, 512], BF16, name="pt_sb")
        r_sb = const.tile([P, 256], BF16, name="r_sb")
        a_sb = const.tile([P, 4, 256], BF16, name="a_sb")
        grouped = const.tile([P, 4, 1024], BF16, name="grouped", align_bytes=256)
        fw = const.tile([P, 4, 256], U32, name="fw", align_bytes=256)
        fs = const.tile([P, 4, 256], U8, name="fs", align_bytes=256)

        def copy_out(engine, dst, src):
            if engine == 0:
                nc.scalar.copy(out=dst, in_=src)
            else:
                nc.vector.tensor_copy(out=dst, in_=src)

        nc.vector.memset(x0[:], 0.0)
        nc.scalar.dma_start(out=x0[0:32, 0:121], in_=x.rearrange("n c h w -> (n c) (h w)"))
        nc.vector.memset(planes[:].bitcast(I32), 0)
        make_identity(nc, ident_bf[:])

        def load_w(g, o0, width, name):
            w = const.tile([P, width], I32, name=name, align_bytes=256)
            src = W_words[g].rearrange("p n t -> p (n t)")[:, 4 * o0 : 4 * (o0 + width)]
            nc.sync.dma_start(out=w[:], in_=src.bitcast(I32))
            return w

        w_h0 = [load_w(0, 0, 2048, "w0_0")]
        for h in range(2):
            for q in range(2):
                nc.sync.dma_start(
                    out=planes[32 * q : 32 * q + 16, h, :].bitcast(I32),
                    in_=W_scales[4 * h : 4 * h + 4, 4 * q : 4 * q + 4, :].bitcast(I32),
                )
        for r in range(4):
            for q in range(2, 4):
                nc.gpsimd.dma_start(
                    out=planes[32 * q + r : 32 * q + 16 : 4, :, :].bitcast(F32),
                    in_=W_scales[:, 4 * q + r, :].rearrange("(h k) n -> k h n", k=4).bitcast(F32),
                )
        make_identity(nc, ident_f[:])
        w_h0.extend([load_w(g, 0, 2048, "w0_%d" % g) for g in range(1, 4)])

        def load_pair(g):
            w = const.tile([P, 2, 2048], I32, name="w0_%d_%d" % (g, g + 1), align_bytes=256)
            src = W_words[g : g + 2].rearrange("g p n t -> p g (n t)")[:, :, 0 : 4 * 2048]
            nc.sync.dma_start(out=w[:], in_=src.bitcast(I32))
            return [w[:, 0, :], w[:, 1, :]]

        w_h0.extend(load_pair(4))
        w_h0.extend(load_pair(6))
        w_h1 = [load_w(g, 2048, 2048, "w1_%d" % g) for g in range(TAIL_G)]

        def load_tail(i):
            o0, width = 2048 + BLOCKS[i][0], BLOCKS[i][1]
            w = const.tile([P, 8 - TAIL_G, width], I32, name="w1_tail_%d" % i, align_bytes=256)
            src = W_words[TAIL_G:8].rearrange("g p n t -> p g (n t)")[:, :, 4 * o0 : 4 * (o0 + width)]
            nc.sync.dma_start(out=w[:], in_=src.bitcast(I32))
            return w

        w_last = [load_tail(i) for i in range(len(BLOCKS))]

        nc.vector.tensor_copy(
            out=sel_a[:].rearrange("q (v j) -> q v j", j=4),
            in_=ident_bf[:].unsqueeze(2).to_broadcast([P, P, 4]),
        )
        ident_ajt = ident_bf[:].rearrange("q (a j t) -> q a j t", a=8, j=4, t=4)
        for t in range(4):
            nc.vector.tensor_copy(
                out=sel_b[:, t, :].rearrange("q (a i j) -> q a i j", a=8, i=16, j=4),
                in_=ident_ajt[:, :, :, t].unsqueeze(2).to_broadcast([P, 8, 16, 4]),
            )

        pt_view = pt_sb[:].rearrange("e (q i) -> e q i", i=16)
        for half in range(2):
            pt_ps = psum.tile([P, 8, P], BF16, name="pt_ps%d" % half, tag="b%d" % half)
            for k in range(8):
                i = 8 * half + k
                off = (i // 4) * 11 + i % 4
                nc.tensor.transpose(pt_ps[:, k, :], x0[:, off : off + P], ident_bf[:])
            copy_out(
                1,
                pt_view[:, :, 8 * half : 8 * half + 8],
                pt_ps[:, :, 0:32].rearrange("e i q -> e q i"),
            )
        r_ps = psum.tile([P, 4, P], BF16, name="r_ps", tag="b2")
        for ghi in range(2):
            for n in range(2):
                s = (n * 16 + ghi * 8) * 16
                nc.tensor.transpose(r_ps[:, ghi * 2 + n, :], pt_sb[:, s : s + P], ident_bf[:])
        nc.vector.tensor_copy(
            out=r_sb[:].rearrange("q (b y z) -> q b y z", b=4, y=8),
            in_=r_ps[:, :, 0:88].rearrange("q b (y w) -> q b y w", w=11)[:, :, :, 0:8],
        )

        a_ps = psum.tile([P, 4, 256], BF16, name="a_ps", tag="b3")
        for glo in range(4):
            nc.tensor.matmul(
                a_ps[:, glo, :], lhsT=sel_a[:, glo * P : (glo + 1) * P], rhs=r_sb[:],
                start=True, stop=True,
            )
        nc.scalar.copy(out=a_sb[:], in_=a_ps[:])
        b_ps = []
        for glo in range(4):
            b = psum.tile([P, 4, 256], BF16, name="b_ps%d" % glo, tag="b%d" % (4 + glo))
            for t in range(4):
                nc.tensor.matmul(
                    b[:, t, :], lhsT=sel_b[:, t, glo * P : (glo + 1) * P], rhs=r_sb[:],
                    start=True, stop=True,
                )
            b_ps.append(b)

        def product(glo):
            nc.vector.tensor_tensor(
                out=grouped[:, glo, :].rearrange("p (c t) -> p c t", t=4),
                in0=a_sb[:, glo, :].unsqueeze(2).to_broadcast([P, 256, 4]),
                in1=b_ps[glo][:].rearrange("p t c -> p c t"),
                op=MULT,
            )

        def quantise(glo):
            nc.vector.quantize_mx(
                out=fw[:, glo, :].bitcast(FP8X4), scales=fs[:, glo, :], in_=grouped[:, glo, :]
            )

        product(0)
        product(1)
        quantise(0)
        product(2)
        quantise(1)
        product(3)
        quantise(2)
        quantise(3)

        def mx_pass(acc, g, w_cols, o0, width=512):
            ghi, glo = g // 4, g % 4
            nc.tensor.matmul_mx(
                out=acc[:],
                lhsT=fw[:, glo, ghi * P : (ghi + 1) * P].bitcast(FP8X4),
                lhsT_scale=fs[:, glo, ghi * P : (ghi + 1) * P],
                rhs=w_cols.bitcast(FP8X4),
                rhs_scale=planes[4 * glo : P, ghi, o0 : o0 + width],
                start=(g == 0),
                stop=(g == 7),
            )

        out_rows = out.rearrange("n o y z -> n o (y z)")

        def evac1(acc, engine, R):
            s = stage_s.tile([P, R, P], F32, name="s", tag="s", align_bytes=256)
            copy_out(engine, s[:], acc[:].rearrange("p (m r) -> p r m", r=R))
            return s

        def back(s, bank, R):
            t_ps = psum.tile([P, R, P], F32, name="t_ps", tag="b%d" % bank)
            for r in range(R):
                nc.tensor.transpose(t_ps[:, r, :], s[:, r, :], ident_f[:])
            return t_ps

        def evac2_store(t_ps, engine, o0, R):
            o_sb = stage_o.tile([P, 2, R, 64], F32, name="o_sb", tag="o", align_bytes=256)
            copy_out(engine, o_sb[:], t_ps[:].rearrange("m r (n l) -> m n r l", n=2))
            nc.sync.dma_start(
                out=out_rows[:, o0 : o0 + P * R, :].rearrange("n (m r) l -> m n (r l)", r=R),
                in_=o_sb[:].rearrange("m n r l -> m n (r l)"),
            )

        acc0 = [psum.tile([P, 512], F32, name="acc0_%d" % j, tag="b%d" % j) for j in range(4)]
        for g in range(8):
            for j in range(4):
                mx_pass(acc0[j], g, w_h0[g][:, 512 * j : 512 * (j + 1)], 512 * j)
        s_all = const.tile([P, 16, P], F32, name="s_all")
        for j in range(4):
            copy_out(
                j % 2,
                s_all[:, :, 32 * j : 32 * (j + 1)],
                acc0[j][:].rearrange("p (m r) -> p r m", r=16),
            )
        o_all = const.tile([P, 2, 16, 64], F32, name="o_all", align_bytes=256)
        t0 = []
        for b in range(4):
            t_ps = psum.tile([P, 4, P], F32, name="t0_ps", tag="b%d" % b)
            for r in range(4):
                nc.tensor.transpose(t_ps[:, r, :], s_all[:, 4 * b + r, :], ident_f[:])
            t0.append(t_ps)
        for b in range(4):
            copy_out(
                b % 2,
                o_all[:, :, 4 * b : 4 * (b + 1), :],
                t0[b][:].rearrange("m r (n l) -> m n r l", n=2),
            )
        nc.sync.dma_start(
            out=out_rows[:, 0:2048, :].rearrange("n (m r) l -> m n (r l)", r=16),
            in_=o_all[:].rearrange("m n r l -> m n (r l)"),
        )

        acc1 = [
            psum.tile([P, BLOCKS[i][1]], F32, name="acc1_%d" % i, tag="b%d" % ACC_BANK[i])
            for i in range(len(BLOCKS))
        ]
        for g in range(TAIL_G):
            for i in range(len(BLOCKS)):
                c0, width = BLOCKS[i]
                mx_pass(acc1[i], g, w_h1[g][:, c0 : c0 + width], 2048 + c0, width)
        s1 = [None] * len(BLOCKS)

        def close(i):
            c0, width = BLOCKS[i]
            for g in range(TAIL_G, 8):
                mx_pass(acc1[i], g, w_last[i][:, g - TAIL_G, :], 2048 + c0, width)
            s1[i] = evac1(acc1[i], i % 2, width // P)

        def finish(i):
            c0, width = BLOCKS[i]
            t_ps = back(s1[i], BACK_BANK[i], width // P)
            evac2_store(t_ps, (i + 1) % 2, 2048 + c0, width // P)

        close(0)
        for i in range(1, len(BLOCKS)):
            close(i)
            finish(i - 1)
        finish(len(BLOCKS) - 1)
